import numpy as np
import ml_dtypes


def mxq(x, axis, fmt="e4m3"):
    dtype, down = {"e4m3": (ml_dtypes.float8_e4m3fn, 7), "e5m2": (ml_dtypes.float8_e5m2, 14)}[fmt]
    v = np.moveaxis(np.asarray(x, np.float32).astype(ml_dtypes.bfloat16).astype(np.float64), axis, -1)
    blocks = v.reshape(v.shape[:-1] + (-1, 32))
    amax = np.abs(blocks).max(-1, keepdims=True)
    byte = np.maximum(np.where(amax > 0, np.frexp(amax)[1] - 1 + 127, 0) - down, 1)
    scale = np.exp2(byte - 127.0)
    codes = (blocks / scale).astype(np.float32).astype(dtype).astype(np.float64)
    return np.moveaxis((codes * scale).reshape(v.shape), -1, axis)


WIDE = False


def mx_kscale(k):
    if not WIDE:
        return np.ones(k)
    levels = np.array([10, -10, 5, -5, 0])
    a = np.random.permutation(np.resize(levels, k // 512 * 4)).reshape(k // 512, 4)
    idx = np.arange(k)
    return np.exp2(a[idx // 512, idx % 128 // 32])


BF16 = ml_dtypes.bfloat16


def bf(x):
    return np.asarray(x, np.float32).astype(BF16)


def f64(x):
    return np.asarray(x).astype(np.float64)


NU, NI, NE, EMB = 192, 320, 512, 384
N = NU + NI
LN_EPS = 1e-5
DENS = 0.01
A_SCALE = (1.5e-4 / ((NE * DENS) ** 2 + N * NE * DENS ** 2 * (1.0 + NE * DENS ** 2))) ** 0.25


def setup_inputs():
    s = mx_kscale(N)
    adj = (np.random.uniform(size=(N, NE)) < DENS) * np.random.uniform(0.5, 1.5, (N, NE)) * A_SCALE
    return {"e_nodes": bf(np.random.standard_normal((N, EMB)) / s[:, None]),
            "adj": bf(adj * s[:, None]),
            "ego_embeddings": bf(np.random.standard_normal((N, EMB))),
            "ln_gamma": bf(1.0 + 0.1 * np.random.standard_normal(EMB)),
            "ln_beta": bf(0.1 * np.random.standard_normal(EMB))}


def reference(e_nodes, adj, ego_embeddings, ln_gamma, ln_beta):
    a = f64(adj)
    m = mxq(a.T, 1, "e4m3") @ mxq(f64(e_nodes), 0, "e4m3")
    h = mxq(a, 1, "e4m3") @ mxq(m, 0, "e4m3")
    mu = h.mean(-1, keepdims=True)
    var = h.var(-1, keepdims=True)
    return (h - mu) * (1.0 / np.sqrt(var + LN_EPS)) * f64(ln_gamma) + f64(ln_beta) + f64(ego_embeddings)

@@ -1,0 +1,233 @@
+import concourse.mybir as mybir
+from concourse.masks import make_identity
+
+BF16 = mybir.dt.bfloat16
+F32 = mybir.dt.float32
+U32 = mybir.dt.uint32
+U8 = mybir.dt.uint8
+FP8X4 = mybir.dt.float8_e4m3fn_x4
+ACT = mybir.ActivationFunctionType
+ALU = mybir.AluOpType
+
+P = 128
+PACK = 4
+NODES = 512
+EDGES = 512
+EMB = 384
+LN_EPS = 1e-5
+
+ROWS = NODES // P
+HALF = EDGES // 2
+F_BLOCKS = EMB // P
+BANK = 512
+
+FLOPS = 2 * 2 * NODES * EDGES * EMB
+
+
+def tile_hgnnmodel_pa_s_kernel(tc, e_nodes, adj, ego_embeddings, ln_gamma, ln_beta, out):
+    nc = tc.nc
+    with tc.tile_pool(name="sbuf", bufs=1) as sbuf, tc.psum_pool(
+        name="psum", bufs=8
+    ) as psum, tc.manual_schedule():
+
+        adj_half = []
+        for u in range(2):
+            half = sbuf.tile([P, ROWS * HALF], BF16, name="adj_half%d" % u)
+            nc.sync.dma_start(
+                out=half[:].rearrange("p (j e) -> p j e", j=ROWS),
+                in_=adj[:, u * HALF : (u + 1) * HALF].rearrange("(p j) e -> p j e", j=ROWS),
+            )
+            adj_half.append(half)
+        e_raw = sbuf.tile([P, ROWS, EMB], BF16)
+        nc.scalar.dma_start(out=e_raw[:], in_=e_nodes.rearrange("(p j) f -> p j f", j=ROWS))
+        ego_raw = sbuf.tile([P, ROWS, EMB], BF16)
+        nc.sync.dma_start(out=ego_raw[:], in_=ego_embeddings.rearrange("(p j) f -> p j f", j=ROWS))
+        beta_all = sbuf.tile([P, EMB], BF16)
+        nc.sync.dma_start(out=beta_all[:], in_=ln_beta.partition_broadcast(P))
+        gamma_all = sbuf.tile([P, EMB], BF16)
+        nc.sync.dma_start(out=gamma_all[:], in_=ln_gamma.partition_broadcast(P))
+
+        ones = sbuf.tile([P, 1], F32)
+        nc.vector.memset(ones[:], 1.0)
+        table_warm = sbuf.tile([P, 1], F32)
+        nc.scalar.activation(out=table_warm[:], in_=ones[:], func=ACT.Abs_reciprocal_sqrt)
+        ident = sbuf.tile([P, P], F32)
+        make_identity(nc, ident[:])
+
+        adj_t = []
+        for c in range(2):
+            bank = psum.tile([P, BANK], F32, name="adj_t%d" % c, tag="bank")
+            for u in range(2):
+                for i in range(2):
+                    j = 2 * c + i
+                    nc.tensor.transpose(
+                        bank[:, (2 * u + i) * P : (2 * u + i + 1) * P],
+                        adj_half[u][:].bitcast(F32)[:, j * P : (j + 1) * P],
+                        ident[:],
+                    )
+            adj_t.append(bank)
+
+        a_grouped = sbuf.tile([P, EDGES * PACK], BF16, align_bytes=64)
+        a_codes = sbuf.tile([P, EDGES], U32, align_bytes=64)
+        a_scales = sbuf.tile([P, EDGES], U8, align_bytes=64)
+        e_grouped = sbuf.tile([P, EMB, PACK], BF16, align_bytes=64)
+        e_codes = sbuf.tile([P, EMB], U32, align_bytes=64)
+        e_scales = sbuf.tile([P, EMB], U8, align_bytes=64)
+        for u in range(2):
+            nc.vector.tensor_copy(
+                out=a_grouped[:, u * HALF * PACK : (u + 1) * HALF * PACK].rearrange(
+                    "p (s q j) -> p s q j", s=2, j=ROWS
+                ),
+                in_=adj_half[u][:].rearrange("p (j q s) -> p s q j", j=ROWS, s=2),
+            )
+        for b in range(F_BLOCKS):
+            f_cols = slice(b * P, (b + 1) * P)
+            nc.scalar.copy(
+                out=e_grouped[:, f_cols, :], in_=e_raw[:, :, f_cols].rearrange("p j f -> p f j")
+            )
+        for u in range(2):
+            nc.vector.quantize_mx(
+                out=a_codes[:, u * HALF : (u + 1) * HALF].bitcast(FP8X4),
+                scales=a_scales[:, u * HALF : (u + 1) * HALF],
+                in_=a_grouped[:, u * HALF * PACK : (u + 1) * HALF * PACK],
+            )
+        for b in range(F_BLOCKS):
+            f_cols = slice(b * P, (b + 1) * P)
+            nc.vector.quantize_mx(
+                out=e_codes[:, f_cols].bitcast(FP8X4),
+                scales=e_scales[:, f_cols],
+                in_=e_grouped[:, f_cols, :].rearrange("p f j -> p (f j)"),
+            )
+
+        m_ps = []
+        for b in range(F_BLOCKS):
+            f_cols = slice(b * P, (b + 1) * P)
+            bank = psum.tile([P, PACK, P], F32, name="m_ps%d" % b, tag="bank")
+            for t in range(PACK):
+                nc.tensor.matmul_mx(
+                    out=bank[:, t, :],
+                    lhsT=a_codes[:, t * P : (t + 1) * P].bitcast(FP8X4),
+                    lhsT_scale=a_scales[:, t * P : (t + 1) * P],
+                    rhs=e_codes[:, f_cols].bitcast(FP8X4),
+                    rhs_scale=e_scales[:, f_cols],
+                    start=True,
+                    stop=True,
+                )
+            m_ps.append(bank)
+
+        b_grouped = sbuf.tile([P, NODES * PACK], BF16, align_bytes=64)
+        b_codes = sbuf.tile([P, NODES], U32, align_bytes=64)
+        b_scales = sbuf.tile([P, NODES], U8, align_bytes=64)
+        for c in range(2):
+            nc.scalar.copy(
+                out=b_grouped[:].bitcast(F32)[:, c * BANK : (c + 1) * BANK].rearrange(
+                    "p (n u) -> p n u", u=2
+                ),
+                in_=adj_t[c][:].rearrange("p (u n) -> p n u", u=2),
+            )
+
+        shift = sbuf.tile([P, ROWS, EMB], F32)
+
+        def join_bias_and_residual(j):
+            nc.vector.tensor_tensor(
+                out=shift[:, j, :], in0=ego_raw[:, j, :], in1=beta_all[:], op=ALU.add
+            )
+
+        join_bias_and_residual(0)
+        for c in range(2):
+            nc.vector.quantize_mx(
+                out=b_codes[:, c * 2 * P : (c + 1) * 2 * P].bitcast(FP8X4),
+                scales=b_scales[:, c * 2 * P : (c + 1) * 2 * P],
+                in_=b_grouped[:, c * 2 * P * PACK : (c + 1) * 2 * P * PACK],
+            )
+
+        m_grouped = sbuf.tile([P, EMB, PACK], BF16, align_bytes=64)
+        m_codes = sbuf.tile([P, EMB], U32, align_bytes=64)
+        m_scales = sbuf.tile([P, EMB], U8, align_bytes=64)
+        h_ps = [psum.tile([P, BANK], F32, name="h_ps%d" % j, tag="bank") for j in range(ROWS)]
+        for b in range(F_BLOCKS):
+            f_cols = slice(b * P, (b + 1) * P)
+            nc.scalar.copy(out=m_grouped[:, f_cols, :], in_=m_ps[b][:].rearrange("p t f -> p f t"))
+            nc.vector.quantize_mx(
+                out=m_codes[:, f_cols].bitcast(FP8X4),
+                scales=m_scales[:, f_cols],
+                in_=m_grouped[:, f_cols, :].rearrange("p f t -> p (f t)"),
+            )
+            join_bias_and_residual(b + 1)
+            for j in range(ROWS):
+                nc.tensor.matmul_mx(
+                    out=h_ps[j][:, f_cols],
+                    lhsT=b_codes[:, j * P : (j + 1) * P].bitcast(FP8X4),
+                    lhsT_scale=b_scales[:, j * P : (j + 1) * P],
+                    rhs=m_codes[:, f_cols].bitcast(FP8X4),
+                    rhs_scale=m_scales[:, f_cols],
+                    start=True,
+                    stop=True,
+                )
+
+        neg_mean = sbuf.tile([P, ROWS], F32)
+        sq_sum = sbuf.tile([P, ROWS], F32)
+        var_eps = sbuf.tile([P, ROWS], F32)
+        rstd = sbuf.tile([P, ROWS], F32)
+        h_scaled = sbuf.tile([P, ROWS, EMB], F32)
+        squares = sbuf.tile([P, ROWS, EMB], F32)
+        centred = sbuf.tile([P, ROWS, EMB], F32)
+        result = sbuf.tile([P, ROWS, EMB], F32)
+        out_rows = out.rearrange("(p j) f -> p j f", j=ROWS)
+
+        def mean_and_centre(j):
+            nc.scalar.activation(
+                out=h_scaled[:, j, :],
+                in_=h_ps[j][:, 0:EMB],
+                func=ACT.Copy,
+                scale=-1.0 / EMB,
+                accum_out=neg_mean[:, j : j + 1],
+            )
+            nc.vector.scalar_tensor_tensor(
+                out=centred[:, j, :],
+                in0=h_ps[j][:, 0:EMB],
+                scalar=neg_mean[:, j : j + 1],
+                in1=gamma_all[:],
+                op0=ALU.add,
+                op1=ALU.mult,
+            )
+
+        def variance(j):
+            nc.scalar.activation(
+                out=squares[:, j, :],
+                in_=h_scaled[:, j, :],
+                func=ACT.Square,
+                scale=-1.0 * EMB,
+                bias=neg_mean[:, j : j + 1],
+                accum_out=sq_sum[:, j : j + 1],
+            )
+            nc.vector.tensor_scalar(
+                out=var_eps[:, j : j + 1],
+                in0=sq_sum[:, j : j + 1],
+                scalar1=1.0 / EMB,
+                scalar2=LN_EPS,
+                op0=ALU.mult,
+                op1=ALU.add,
+            )
+
+        def normalise_and_store(j):
+            nc.scalar.activation(
+                out=rstd[:, j : j + 1], in_=var_eps[:, j : j + 1], func=ACT.Abs_reciprocal_sqrt
+            )
+            nc.vector.scalar_tensor_tensor(
+                out=result[:, j, :],
+                in0=centred[:, j, :],
+                scalar=rstd[:, j : j + 1],
+                in1=shift[:, j, :],
+                op0=ALU.mult,
+                op1=ALU.add,
+            )
+            nc.sync.dma_start(out=out_rows[:, j, :], in_=result[:, j, :])
+
+        for step in range(ROWS + 2):
+            if step < ROWS:
+                mean_and_centre(step)
+            if step >= 2:
+                normalise_and_store(step - 2)
+            if 1 <= step <= ROWS:
+                variance(step - 1)

@@ -42,10 +42,14 @@ def tile_hgnnmodel_pa_s_kernel(tc, e_nodes, adj, ego_embeddings, ln_gamma, ln_be
         nc.scalar.dma_start(out=e_raw[:], in_=e_nodes.rearrange("(p j) f -> p j f", j=ROWS))
         ego_raw = sbuf.tile([P, ROWS, EMB], BF16)
         nc.sync.dma_start(out=ego_raw[:], in_=ego_embeddings.rearrange("(p j) f -> p j f", j=ROWS))
-        beta_all = sbuf.tile([P, EMB], BF16)
-        nc.sync.dma_start(out=beta_all[:], in_=ln_beta.partition_broadcast(P))
-        gamma_all = sbuf.tile([P, EMB], BF16)
-        nc.sync.dma_start(out=gamma_all[:], in_=ln_gamma.partition_broadcast(P))
+        gain_bias_row = sbuf.tile([P, 2, BANK], BF16)
+        nc.vector.memset(gain_bias_row[:], 0.0)
+        nc.scalar.dma_start(
+            out=gain_bias_row[0:1, 0, 0:EMB], in_=ln_gamma.rearrange("(o f) -> o f", o=1)
+        )
+        nc.scalar.dma_start(
+            out=gain_bias_row[0:1, 1, 0:EMB], in_=ln_beta.rearrange("(o f) -> o f", o=1)
+        )
 
         ones = sbuf.tile([P, 1], F32)
         nc.vector.memset(ones[:], 1.0)
@@ -53,6 +57,8 @@ def tile_hgnnmodel_pa_s_kernel(tc, e_nodes, adj, ego_embeddings, ln_gamma, ln_be
         nc.scalar.activation(out=table_warm[:], in_=ones[:], func=ACT.Abs_reciprocal_sqrt)
         ident = sbuf.tile([P, P], F32)
         make_identity(nc, ident[:])
+        all_ones = sbuf.tile([P, P], BF16)
+        nc.vector.memset(all_ones[:], 1.0)
 
         adj_t = []
         for c in range(2):
@@ -66,6 +72,16 @@ def tile_hgnnmodel_pa_s_kernel(tc, e_nodes, adj, ego_embeddings, ln_gamma, ln_be
                         ident[:],
                     )
             adj_t.append(bank)
+
+        gain_bias_ps = psum.tile([P, 2, BANK], BF16, tag="bank")
+        for g in range(2):
+            nc.tensor.matmul(
+                out=gain_bias_ps[:, g, :],
+                lhsT=all_ones[:],
+                rhs=gain_bias_row[:, g, :],
+                start=True,
+                stop=True,
+            )
 
         a_grouped = sbuf.tile([P, EDGES * PACK], BF16, align_bytes=64)
         a_codes = sbuf.tile([P, EDGES], U32, align_bytes=64)
@@ -126,11 +142,16 @@ def tile_hgnnmodel_pa_s_kernel(tc, e_nodes, adj, ego_embeddings, ln_gamma, ln_be
                 in_=adj_t[c][:].rearrange("p (u n) -> p n u", u=2),
             )
 
+        gain_bias = sbuf.tile([P, 2, EMB], BF16)
+        nc.vector.tensor_copy(out=gain_bias[:], in_=gain_bias_ps[:, :, 0:EMB])
+        gamma_all = gain_bias[:, 0, :]
+        beta_all = gain_bias[:, 1, :]
+
         shift = sbuf.tile([P, ROWS, EMB], F32)
 
         def join_bias_and_residual(j):
             nc.vector.tensor_tensor(
-                out=shift[:, j, :], in0=ego_raw[:, j, :], in1=beta_all[:], op=ALU.add
+                out=shift[:, j, :], in0=ego_raw[:, j, :], in1=beta_all, op=ALU.add
             )
 
         join_bias_and_residual(0)
@@ -187,7 +208,7 @@ def tile_hgnnmodel_pa_s_kernel(tc, e_nodes, adj, ego_embeddings, ln_gamma, ln_be
                 out=centred[:, j, :],
                 in0=h_ps[j][:, 0:EMB],
                 scalar=neg_mean[:, j : j + 1],
-                in1=gamma_all[:],
+                in1=gamma_all,
                 op0=ALU.add,
                 op1=ALU.mult,
             )

@@ -30,6 +30,16 @@ def tile_hgnnmodel_pa_s_kernel(tc, e_nodes, adj, ego_embeddings, ln_gamma, ln_be
         name="psum", bufs=8
     ) as psum, tc.manual_schedule():
 
+        e_raw = sbuf.tile([P, ROWS, EMB], BF16)
+        nc.sync.dma_start(out=e_raw[:], in_=e_nodes.rearrange("(p j) f -> p j f", j=ROWS))
+        gain_bias_row = sbuf.tile([P, 2, BANK], BF16)
+        nc.vector.memset(gain_bias_row[:], 0.0)
+        nc.sync.dma_start(
+            out=gain_bias_row[0:1, 0, 0:EMB], in_=ln_gamma.rearrange("(o f) -> o f", o=1)
+        )
+        nc.sync.dma_start(
+            out=gain_bias_row[0:1, 1, 0:EMB], in_=ln_beta.rearrange("(o f) -> o f", o=1)
+        )
         adj_half = []
         for u in range(2):
             half = sbuf.tile([P, ROWS * HALF], BF16, name="adj_half%d" % u)
@@ -38,27 +48,27 @@ def tile_hgnnmodel_pa_s_kernel(tc, e_nodes, adj, ego_embeddings, ln_gamma, ln_be
                 in_=adj[:, u * HALF : (u + 1) * HALF].rearrange("(p j) e -> p j e", j=ROWS),
             )
             adj_half.append(half)
-        e_raw = sbuf.tile([P, ROWS, EMB], BF16)
-        nc.scalar.dma_start(out=e_raw[:], in_=e_nodes.rearrange("(p j) f -> p j f", j=ROWS))
         ego_raw = sbuf.tile([P, ROWS, EMB], BF16)
         nc.sync.dma_start(out=ego_raw[:], in_=ego_embeddings.rearrange("(p j) f -> p j f", j=ROWS))
-        gain_bias_row = sbuf.tile([P, 2, BANK], BF16)
-        nc.vector.memset(gain_bias_row[:], 0.0)
-        nc.scalar.dma_start(
-            out=gain_bias_row[0:1, 0, 0:EMB], in_=ln_gamma.rearrange("(o f) -> o f", o=1)
-        )
-        nc.scalar.dma_start(
-            out=gain_bias_row[0:1, 1, 0:EMB], in_=ln_beta.rearrange("(o f) -> o f", o=1)
-        )
 
-        ones = sbuf.tile([P, 1], F32)
-        nc.vector.memset(ones[:], 1.0)
-        table_warm = sbuf.tile([P, 1], F32)
-        nc.scalar.activation(out=table_warm[:], in_=ones[:], func=ACT.Abs_reciprocal_sqrt)
-        ident = sbuf.tile([P, P], F32)
-        make_identity(nc, ident[:])
         all_ones = sbuf.tile([P, P], BF16)
         nc.vector.memset(all_ones[:], 1.0)
+        neg_half = sbuf.tile([P, 1], F32)
+        nc.vector.memset(neg_half[:], -0.5)
+        table_warm = sbuf.tile([P, 1], F32)
+        nc.scalar.activation(out=table_warm[:], in_=neg_half[:], func=ACT.Copy)
+        ident = sbuf.tile([P, P], F32)
+        make_identity(nc, ident[:])
+
+        gain_bias_ps = psum.tile([P, 2, BANK], BF16, tag="bank")
+        for g in range(2):
+            nc.tensor.matmul(
+                out=gain_bias_ps[:, g, :],
+                lhsT=all_ones[:],
+                rhs=gain_bias_row[:, g, :],
+                start=True,
+                stop=True,
+            )
 
         adj_t = []
         for c in range(2):
@@ -72,16 +82,6 @@ def tile_hgnnmodel_pa_s_kernel(tc, e_nodes, adj, ego_embeddings, ln_gamma, ln_be
                         ident[:],
                     )
             adj_t.append(bank)
-
-        gain_bias_ps = psum.tile([P, 2, BANK], BF16, tag="bank")
-        for g in range(2):
-            nc.tensor.matmul(
-                out=gain_bias_ps[:, g, :],
-                lhsT=all_ones[:],
-                rhs=gain_bias_row[:, g, :],
-                start=True,
-                stop=True,
-            )
 
         a_grouped = sbuf.tile([P, EDGES * PACK], BF16, align_bytes=64)
         a_codes = sbuf.tile([P, EDGES], U32, align_bytes=64)
@@ -99,7 +99,8 @@ def tile_hgnnmodel_pa_s_kernel(tc, e_nodes, adj, ego_embeddings, ln_gamma, ln_be
         for b in range(F_BLOCKS):
             f_cols = slice(b * P, (b + 1) * P)
             nc.scalar.copy(
-                out=e_grouped[:, f_cols, :], in_=e_raw[:, :, f_cols].rearrange("p j f -> p f j")
+                out=e_grouped[:, f_cols, :].rearrange("p (c i) j -> p c j i", i=4),
+                in_=e_raw[:, :, f_cols].rearrange("p j (c i) -> p c j i", i=4),
             )
         for u in range(2):
             nc.vector.quantize_mx(
@@ -186,6 +187,7 @@ def tile_hgnnmodel_pa_s_kernel(tc, e_nodes, adj, ego_embeddings, ln_gamma, ln_be
                     stop=True,
                 )
 
+        mean_var = sbuf.tile([P, 2], F32)
         neg_mean = sbuf.tile([P, ROWS], F32)
         sq_sum = sbuf.tile([P, ROWS], F32)
         var_eps = sbuf.tile([P, ROWS], F32)
@@ -196,7 +198,7 @@ def tile_hgnnmodel_pa_s_kernel(tc, e_nodes, adj, ego_embeddings, ln_gamma, ln_be
         result = sbuf.tile([P, ROWS, EMB], F32)
         out_rows = out.rearrange("(p j) f -> p j f", j=ROWS)
 
-        def mean_and_centre(j):
+        def mean_on_scalar(j):
             nc.scalar.activation(
                 out=h_scaled[:, j, :],
                 in_=h_ps[j][:, 0:EMB],
@@ -204,16 +206,8 @@ def tile_hgnnmodel_pa_s_kernel(tc, e_nodes, adj, ego_embeddings, ln_gamma, ln_be
                 scale=-1.0 / EMB,
                 accum_out=neg_mean[:, j : j + 1],
             )
-            nc.vector.scalar_tensor_tensor(
-                out=centred[:, j, :],
-                in0=h_ps[j][:, 0:EMB],
-                scalar=neg_mean[:, j : j + 1],
-                in1=gamma_all,
-                op0=ALU.add,
-                op1=ALU.mult,
-            )
 
-        def variance(j):
+        def squares_on_scalar(j):
             nc.scalar.activation(
                 out=squares[:, j, :],
                 in_=h_scaled[:, j, :],
@@ -222,19 +216,31 @@ def tile_hgnnmodel_pa_s_kernel(tc, e_nodes, adj, ego_embeddings, ln_gamma, ln_be
                 bias=neg_mean[:, j : j + 1],
                 accum_out=sq_sum[:, j : j + 1],
             )
-            nc.vector.tensor_scalar(
+
+        def centre(j, offset, op):
+            nc.vector.scalar_tensor_tensor(
+                out=centred[:, j, :],
+                in0=h_ps[j][:, 0:EMB],
+                scalar=offset,
+                in1=gamma_all,
+                op0=op,
+                op1=ALU.mult,
+            )
+
+        def inverse_std(j, spread, factor):
+            nc.gpsimd.tensor_scalar(
                 out=var_eps[:, j : j + 1],
-                in0=sq_sum[:, j : j + 1],
-                scalar1=1.0 / EMB,
+                in0=spread,
+                scalar1=factor,
                 scalar2=LN_EPS,
                 op0=ALU.mult,
                 op1=ALU.add,
             )
-
-        def normalise_and_store(j):
-            nc.scalar.activation(
-                out=rstd[:, j : j + 1], in_=var_eps[:, j : j + 1], func=ACT.Abs_reciprocal_sqrt
+            nc.gpsimd.tensor_tensor(
+                out=rstd[:, j : j + 1], in0=var_eps[:, j : j + 1], in1=neg_half[:], op=ALU.pow
             )
+
+        def finish(j):
             nc.vector.scalar_tensor_tensor(
                 out=result[:, j, :],
                 in0=centred[:, j, :],
@@ -245,10 +251,17 @@ def tile_hgnnmodel_pa_s_kernel(tc, e_nodes, adj, ego_embeddings, ln_gamma, ln_be
             )
             nc.sync.dma_start(out=out_rows[:, j, :], in_=result[:, j, :])
 
-        for step in range(ROWS + 2):
-            if step < ROWS:
-                mean_and_centre(step)
-            if step >= 2:
-                normalise_and_store(step - 2)
-            if 1 <= step <= ROWS:
-                variance(step - 1)
+        bn_parts = sbuf.tile([P, 6], F32)
+        nc.vector.bn_stats(out=bn_parts[:], in_=h_ps[0][:, 0:EMB])
+        nc.vector.bn_aggr(out=mean_var[:], in_=bn_parts[:])
+        centre(0, mean_var[:, 0:1], ALU.subtract)
+        inverse_std(0, mean_var[:, 1:2], 1.0)
+        mean_on_scalar(1)
+        for j in range(1, ROWS):
+            if j + 1 < ROWS:
+                mean_on_scalar(j + 1)
+            centre(j, neg_mean[:, j : j + 1], ALU.add)
+            squares_on_scalar(j)
+            inverse_std(j, sq_sum[:, j : j + 1], 1.0 / EMB)
+            finish(j - 1)
+        finish(ROWS - 1)

@@ -53,10 +53,12 @@ def tile_hgnnmodel_pa_s_kernel(tc, e_nodes, adj, ego_embeddings, ln_gamma, ln_be
 
         all_ones = sbuf.tile([P, P], BF16)
         nc.vector.memset(all_ones[:], 1.0)
-        neg_half = sbuf.tile([P, 1], F32)
-        nc.vector.memset(neg_half[:], -0.5)
+        one = sbuf.tile([P, 1], F32)
+        nc.vector.memset(one[:], 1.0)
+        eps = sbuf.tile([P, 1], F32)
+        nc.vector.tensor_scalar(out=eps[:], in0=one[:], scalar1=LN_EPS, scalar2=None, op0=ALU.mult)
         table_warm = sbuf.tile([P, 1], F32)
-        nc.scalar.activation(out=table_warm[:], in_=neg_half[:], func=ACT.Copy)
+        nc.scalar.activation(out=table_warm[:], in_=one[:], func=ACT.Abs_reciprocal_sqrt)
         ident = sbuf.tile([P, P], F32)
         make_identity(nc, ident[:])
 
@@ -190,7 +192,6 @@ def tile_hgnnmodel_pa_s_kernel(tc, e_nodes, adj, ego_embeddings, ln_gamma, ln_be
         mean_var = sbuf.tile([P, 2], F32)
         neg_mean = sbuf.tile([P, ROWS], F32)
         sq_sum = sbuf.tile([P, ROWS], F32)
-        var_eps = sbuf.tile([P, ROWS], F32)
         rstd = sbuf.tile([P, ROWS], F32)
         h_scaled = sbuf.tile([P, ROWS, EMB], F32)
         squares = sbuf.tile([P, ROWS, EMB], F32)
@@ -228,16 +229,12 @@ def tile_hgnnmodel_pa_s_kernel(tc, e_nodes, adj, ego_embeddings, ln_gamma, ln_be
             )
 
         def inverse_std(j, spread, factor):
-            nc.gpsimd.tensor_scalar(
-                out=var_eps[:, j : j + 1],
-                in0=spread,
-                scalar1=factor,
-                scalar2=LN_EPS,
-                op0=ALU.mult,
-                op1=ALU.add,
-            )
-            nc.gpsimd.tensor_tensor(
-                out=rstd[:, j : j + 1], in0=var_eps[:, j : j + 1], in1=neg_half[:], op=ALU.pow
+            nc.scalar.activation(
+                out=rstd[:, j : j + 1],
+                in_=spread,
+                func=ACT.Abs_reciprocal_sqrt,
+                scale=factor,
+                bias=eps[:],
             )
 
         def finish(j):
@@ -255,8 +252,8 @@ def tile_hgnnmodel_pa_s_kernel(tc, e_nodes, adj, ego_embeddings, ln_gamma, ln_be
         nc.vector.bn_stats(out=bn_parts[:], in_=h_ps[0][:, 0:EMB])
         nc.vector.bn_aggr(out=mean_var[:], in_=bn_parts[:])
         centre(0, mean_var[:, 0:1], ALU.subtract)
-        inverse_std(0, mean_var[:, 1:2], 1.0)
         mean_on_scalar(1)
+        inverse_std(0, mean_var[:, 1:2], 1.0)
         for j in range(1, ROWS):
             if j + 1 < ROWS:
                 mean_on_scalar(j + 1)

@@ -62,6 +62,7 @@ def tile_hgnnmodel_pa_s_kernel(tc, e_nodes, adj, ego_embeddings, ln_gamma, ln_be
         ident = sbuf.tile([P, P], F32)
         make_identity(nc, ident[:])
 
+        adj_t = [psum.tile([P, BANK], F32, name="adj_t%d" % c, tag="bank") for c in range(2)]
         gain_bias_ps = psum.tile([P, 2, BANK], BF16, tag="bank")
         for g in range(2):
             nc.tensor.matmul(
@@ -72,18 +73,15 @@ def tile_hgnnmodel_pa_s_kernel(tc, e_nodes, adj, ego_embeddings, ln_gamma, ln_be
                 stop=True,
             )
 
-        adj_t = []
         for c in range(2):
-            bank = psum.tile([P, BANK], F32, name="adj_t%d" % c, tag="bank")
             for u in range(2):
                 for i in range(2):
                     j = 2 * c + i
                     nc.tensor.transpose(
-                        bank[:, (2 * u + i) * P : (2 * u + i + 1) * P],
+                        adj_t[c][:, (2 * u + i) * P : (2 * u + i + 1) * P],
                         adj_half[u][:].bitcast(F32)[:, j * P : (j + 1) * P],
                         ident[:],
                     )
-            adj_t.append(bank)
 
         a_grouped = sbuf.tile([P, EDGES * PACK], BF16, align_bytes=64)
         a_codes = sbuf.tile([P, EDGES], U32, align_bytes=64)
@@ -104,14 +102,14 @@ def tile_hgnnmodel_pa_s_kernel(tc, e_nodes, adj, ego_embeddings, ln_gamma, ln_be
                 out=e_grouped[:, f_cols, :].rearrange("p (c i) j -> p c j i", i=4),
                 in_=e_raw[:, :, f_cols].rearrange("p j (c i) -> p c j i", i=4),
             )
-        for u in range(2):
-            nc.vector.quantize_mx(
-                out=a_codes[:, u * HALF : (u + 1) * HALF].bitcast(FP8X4),
-                scales=a_scales[:, u * HALF : (u + 1) * HALF],
-                in_=a_grouped[:, u * HALF * PACK : (u + 1) * HALF * PACK],
-            )
         for b in range(F_BLOCKS):
             f_cols = slice(b * P, (b + 1) * P)
+            if b < 2:
+                nc.vector.quantize_mx(
+                    out=a_codes[:, b * HALF : (b + 1) * HALF].bitcast(FP8X4),
+                    scales=a_scales[:, b * HALF : (b + 1) * HALF],
+                    in_=a_grouped[:, b * HALF * PACK : (b + 1) * HALF * PACK],
+                )
             nc.vector.quantize_mx(
                 out=e_codes[:, f_cols].bitcast(FP8X4),
                 scales=e_scales[:, f_cols],
@@ -145,19 +143,6 @@ def tile_hgnnmodel_pa_s_kernel(tc, e_nodes, adj, ego_embeddings, ln_gamma, ln_be
                 in_=adj_t[c][:].rearrange("p (u n) -> p n u", u=2),
             )
 
-        gain_bias = sbuf.tile([P, 2, EMB], BF16)
-        nc.vector.tensor_copy(out=gain_bias[:], in_=gain_bias_ps[:, :, 0:EMB])
-        gamma_all = gain_bias[:, 0, :]
-        beta_all = gain_bias[:, 1, :]
-
-        shift = sbuf.tile([P, ROWS, EMB], F32)
-
-        def join_bias_and_residual(j):
-            nc.vector.tensor_tensor(
-                out=shift[:, j, :], in0=ego_raw[:, j, :], in1=beta_all, op=ALU.add
-            )
-
-        join_bias_and_residual(0)
         for c in range(2):
             nc.vector.quantize_mx(
                 out=b_codes[:, c * 2 * P : (c + 1) * 2 * P].bitcast(FP8X4),
@@ -169,6 +154,7 @@ def tile_hgnnmodel_pa_s_kernel(tc, e_nodes, adj, ego_embeddings, ln_gamma, ln_be
         m_codes = sbuf.tile([P, EMB], U32, align_bytes=64)
         m_scales = sbuf.tile([P, EMB], U8, align_bytes=64)
         h_ps = [psum.tile([P, BANK], F32, name="h_ps%d" % j, tag="bank") for j in range(ROWS)]
+        shift = sbuf.tile([P, ROWS, EMB], F32)
         for b in range(F_BLOCKS):
             f_cols = slice(b * P, (b + 1) * P)
             nc.scalar.copy(out=m_grouped[:, f_cols, :], in_=m_ps[b][:].rearrange("p t f -> p f t"))
@@ -177,7 +163,13 @@ def tile_hgnnmodel_pa_s_kernel(tc, e_nodes, adj, ego_embeddings, ln_gamma, ln_be
                 scales=m_scales[:, f_cols],
                 in_=m_grouped[:, f_cols, :].rearrange("p f t -> p (f t)"),
             )
-            join_bias_and_residual(b + 1)
+            if b < 2:
+                nc.vector.tensor_tensor(
+                    out=shift[:, b, :],
+                    in0=ego_raw[:, b, :],
+                    in1=gain_bias_ps[:, 1, 0:EMB],
+                    op=ALU.add,
+                )
             for j in range(ROWS):
                 nc.tensor.matmul_mx(
                     out=h_ps[j][:, f_cols],
@@ -188,6 +180,13 @@ def tile_hgnnmodel_pa_s_kernel(tc, e_nodes, adj, ego_embeddings, ln_gamma, ln_be
                     start=True,
                     stop=True,
                 )
+
+        gain_bias = sbuf.tile([P, 2, EMB], BF16)
+        nc.scalar.copy(out=gain_bias[:], in_=gain_bias_ps[:, :, 0:EMB])
+        for j in range(2, ROWS):
+            nc.gpsimd.tensor_tensor(
+                out=shift[:, j, :], in0=ego_raw[:, j, :], in1=gain_bias[:, 1, :], op=ALU.add
+            )
 
         mean_var = sbuf.tile([P, 2], F32)
         neg_mean = sbuf.tile([P, ROWS], F32)
@@ -223,7 +222,7 @@ def tile_hgnnmodel_pa_s_kernel(tc, e_nodes, adj, ego_embeddings, ln_gamma, ln_be
                 out=centred[:, j, :],
                 in0=h_ps[j][:, 0:EMB],
                 scalar=offset,
-                in1=gamma_all,
+                in1=gain_bias[:, 0, :],
                 op0=op,
                 op1=ALU.mult,
             )
@@ -252,13 +251,12 @@ def tile_hgnnmodel_pa_s_kernel(tc, e_nodes, adj, ego_embeddings, ln_gamma, ln_be
         nc.vector.bn_stats(out=bn_parts[:], in_=h_ps[0][:, 0:EMB])
         nc.vector.bn_aggr(out=mean_var[:], in_=bn_parts[:])
         centre(0, mean_var[:, 0:1], ALU.subtract)
-        mean_on_scalar(1)
+        for j in range(1, ROWS):
+            mean_on_scalar(j)
+            centre(j, neg_mean[:, j : j + 1], ALU.add)
         inverse_std(0, mean_var[:, 1:2], 1.0)
         for j in range(1, ROWS):
-            if j + 1 < ROWS:
-                mean_on_scalar(j + 1)
-            centre(j, neg_mean[:, j : j + 1], ALU.add)
             squares_on_scalar(j)
             inverse_std(j, sq_sum[:, j : j + 1], 1.0 / EMB)
-            finish(j - 1)
-        finish(ROWS - 1)
+        for j in range(ROWS):
+            finish(j)

@@ -30,26 +30,20 @@ def tile_hgnnmodel_pa_s_kernel(tc, e_nodes, adj, ego_embeddings, ln_gamma, ln_be
         name="psum", bufs=8
     ) as psum, tc.manual_schedule():
 
+        adj_raw = sbuf.tile([P, ROWS, EDGES], BF16)
+        nc.sync.dma_start(out=adj_raw[:], in_=adj.rearrange("(p j) e -> p j e", j=ROWS))
         e_raw = sbuf.tile([P, ROWS, EMB], BF16)
         nc.sync.dma_start(out=e_raw[:], in_=e_nodes.rearrange("(p j) f -> p j f", j=ROWS))
-        gain_bias_row = sbuf.tile([P, 2, BANK], BF16)
-        nc.vector.memset(gain_bias_row[:], 0.0)
-        nc.sync.dma_start(
-            out=gain_bias_row[0:1, 0, 0:EMB], in_=ln_gamma.rearrange("(o f) -> o f", o=1)
-        )
-        nc.sync.dma_start(
-            out=gain_bias_row[0:1, 1, 0:EMB], in_=ln_beta.rearrange("(o f) -> o f", o=1)
-        )
-        adj_half = []
-        for u in range(2):
-            half = sbuf.tile([P, ROWS * HALF], BF16, name="adj_half%d" % u)
-            nc.sync.dma_start(
-                out=half[:].rearrange("p (j e) -> p j e", j=ROWS),
-                in_=adj[:, u * HALF : (u + 1) * HALF].rearrange("(p j) e -> p j e", j=ROWS),
-            )
-            adj_half.append(half)
         ego_raw = sbuf.tile([P, ROWS, EMB], BF16)
         nc.sync.dma_start(out=ego_raw[:], in_=ego_embeddings.rearrange("(p j) f -> p j f", j=ROWS))
+        gain_bias_row = sbuf.tile([P, 2, EMB], BF16)
+        nc.vector.memset(gain_bias_row[:].rearrange("p g f -> p (g f)").bitcast(F32), 0.0)
+        nc.scalar.dma_start(
+            out=gain_bias_row[0:1, 0, :], in_=ln_gamma.rearrange("(o f) -> o f", o=1)
+        )
+        nc.scalar.dma_start(
+            out=gain_bias_row[0:1, 1, :], in_=ln_beta.rearrange("(o f) -> o f", o=1)
+        )
 
         all_ones = sbuf.tile([P, P], BF16)
         nc.vector.memset(all_ones[:], 1.0)
@@ -62,26 +56,27 @@ def tile_hgnnmodel_pa_s_kernel(tc, e_nodes, adj, ego_embeddings, ln_gamma, ln_be
         ident = sbuf.tile([P, P], F32)
         make_identity(nc, ident[:])
 
+        adj_words = adj_raw[:].rearrange("p j e -> p (j e)").bitcast(F32)
         adj_t = [psum.tile([P, BANK], F32, name="adj_t%d" % c, tag="bank") for c in range(2)]
-        gain_bias_ps = psum.tile([P, 2, BANK], BF16, tag="bank")
-        for g in range(2):
-            nc.tensor.matmul(
-                out=gain_bias_ps[:, g, :],
-                lhsT=all_ones[:],
-                rhs=gain_bias_row[:, g, :],
-                start=True,
-                stop=True,
-            )
-
         for c in range(2):
             for u in range(2):
                 for i in range(2):
                     j = 2 * c + i
                     nc.tensor.transpose(
                         adj_t[c][:, (2 * u + i) * P : (2 * u + i + 1) * P],
-                        adj_half[u][:].bitcast(F32)[:, j * P : (j + 1) * P],
+                        adj_words[:, (2 * j + u) * P : (2 * j + u + 1) * P],
                         ident[:],
                     )
+
+        gain_bias_ps = psum.tile([P, 2, BANK], BF16, tag="bank")
+        for g in range(2):
+            nc.tensor.matmul(
+                out=gain_bias_ps[:, g, 0:EMB],
+                lhsT=all_ones[:],
+                rhs=gain_bias_row[:, g, :],
+                start=True,
+                stop=True,
+            )
 
         a_grouped = sbuf.tile([P, EDGES * PACK], BF16, align_bytes=64)
         a_codes = sbuf.tile([P, EDGES], U32, align_bytes=64)
@@ -94,7 +89,7 @@ def tile_hgnnmodel_pa_s_kernel(tc, e_nodes, adj, ego_embeddings, ln_gamma, ln_be
                 out=a_grouped[:, u * HALF * PACK : (u + 1) * HALF * PACK].rearrange(
                     "p (s q j) -> p s q j", s=2, j=ROWS
                 ),
-                in_=adj_half[u][:].rearrange("p (j q s) -> p s q j", j=ROWS, s=2),
+                in_=adj_raw[:, :, u * HALF : (u + 1) * HALF].rearrange("p j (q s) -> p s q j", s=2),
             )
         for b in range(F_BLOCKS):
             f_cols = slice(b * P, (b + 1) * P)

@@ -19,6 +19,7 @@ LN_EPS = 1e-5
 ROWS = NODES // P
 HALF = EDGES // 2
 F_BLOCKS = EMB // P
+WARM_UPS = 3
 BANK = 512
 
 FLOPS = 2 * 2 * NODES * EDGES * EMB
@@ -32,18 +33,18 @@ def tile_hgnnmodel_pa_s_kernel(tc, e_nodes, adj, ego_embeddings, ln_gamma, ln_be
 
         adj_raw = sbuf.tile([P, ROWS, EDGES], BF16)
         nc.sync.dma_start(out=adj_raw[:], in_=adj.rearrange("(p j) e -> p j e", j=ROWS))
+        gain_bias_row = sbuf.tile([P, 2, EMB], BF16)
+        nc.vector.memset(gain_bias_row[:].rearrange("p g f -> p (g f)").bitcast(F32), 0.0)
+        nc.sync.dma_start(
+            out=gain_bias_row[0:1, 0, :], in_=ln_gamma.rearrange("(o f) -> o f", o=1)
+        )
+        nc.sync.dma_start(
+            out=gain_bias_row[0:1, 1, :], in_=ln_beta.rearrange("(o f) -> o f", o=1)
+        )
         e_raw = sbuf.tile([P, ROWS, EMB], BF16)
         nc.sync.dma_start(out=e_raw[:], in_=e_nodes.rearrange("(p j) f -> p j f", j=ROWS))
         ego_raw = sbuf.tile([P, ROWS, EMB], BF16)
         nc.sync.dma_start(out=ego_raw[:], in_=ego_embeddings.rearrange("(p j) f -> p j f", j=ROWS))
-        gain_bias_row = sbuf.tile([P, 2, EMB], BF16)
-        nc.vector.memset(gain_bias_row[:].rearrange("p g f -> p (g f)").bitcast(F32), 0.0)
-        nc.scalar.dma_start(
-            out=gain_bias_row[0:1, 0, :], in_=ln_gamma.rearrange("(o f) -> o f", o=1)
-        )
-        nc.scalar.dma_start(
-            out=gain_bias_row[0:1, 1, :], in_=ln_beta.rearrange("(o f) -> o f", o=1)
-        )
 
         all_ones = sbuf.tile([P, P], BF16)
         nc.vector.memset(all_ones[:], 1.0)
@@ -55,6 +56,12 @@ def tile_hgnnmodel_pa_s_kernel(tc, e_nodes, adj, ego_embeddings, ln_gamma, ln_be
         nc.scalar.activation(out=table_warm[:], in_=one[:], func=ACT.Abs_reciprocal_sqrt)
         ident = sbuf.tile([P, P], F32)
         make_identity(nc, ident[:])
+
+        warm_ps = psum.tile([P, BANK], F32, tag="bank")
+        for i in range(WARM_UPS):
+            nc.tensor.matmul(
+                out=warm_ps[:, i * P : (i + 1) * P], lhsT=ident[:], rhs=ident[:], start=True, stop=True
+            )
 
         adj_words = adj_raw[:].rearrange("p j e -> p (j e)").bitcast(F32)
         adj_t = [psum.tile([P, BANK], F32, name="adj_t%d" % c, tag="bank") for c in range(2)]
@@ -84,53 +91,31 @@ def tile_hgnnmodel_pa_s_kernel(tc, e_nodes, adj, ego_embeddings, ln_gamma, ln_be
         e_grouped = sbuf.tile([P, EMB, PACK], BF16, align_bytes=64)
         e_codes = sbuf.tile([P, EMB], U32, align_bytes=64)
         e_scales = sbuf.tile([P, EMB], U8, align_bytes=64)
-        for u in range(2):
-            nc.vector.tensor_copy(
-                out=a_grouped[:, u * HALF * PACK : (u + 1) * HALF * PACK].rearrange(
-                    "p (s q j) -> p s q j", s=2, j=ROWS
-                ),
-                in_=adj_raw[:, :, u * HALF : (u + 1) * HALF].rearrange("p j (q s) -> p s q j", s=2),
-            )
-        for b in range(F_BLOCKS):
-            f_cols = slice(b * P, (b + 1) * P)
-            nc.scalar.copy(
-                out=e_grouped[:, f_cols, :].rearrange("p (c i) j -> p c j i", i=4),
-                in_=e_raw[:, :, f_cols].rearrange("p j (c i) -> p c j i", i=4),
-            )
-        for b in range(F_BLOCKS):
-            f_cols = slice(b * P, (b + 1) * P)
-            if b < 2:
-                nc.vector.quantize_mx(
-                    out=a_codes[:, b * HALF : (b + 1) * HALF].bitcast(FP8X4),
-                    scales=a_scales[:, b * HALF : (b + 1) * HALF],
-                    in_=a_grouped[:, b * HALF * PACK : (b + 1) * HALF * PACK],
-                )
-            nc.vector.quantize_mx(
-                out=e_codes[:, f_cols].bitcast(FP8X4),
-                scales=e_scales[:, f_cols],
-                in_=e_grouped[:, f_cols, :].rearrange("p f j -> p (f j)"),
-            )
-
-        m_ps = []
-        for b in range(F_BLOCKS):
-            f_cols = slice(b * P, (b + 1) * P)
-            bank = psum.tile([P, PACK, P], F32, name="m_ps%d" % b, tag="bank")
-            for t in range(PACK):
-                nc.tensor.matmul_mx(
-                    out=bank[:, t, :],
-                    lhsT=a_codes[:, t * P : (t + 1) * P].bitcast(FP8X4),
-                    lhsT_scale=a_scales[:, t * P : (t + 1) * P],
-                    rhs=e_codes[:, f_cols].bitcast(FP8X4),
-                    rhs_scale=e_scales[:, f_cols],
-                    start=True,
-                    stop=True,
-                )
-            m_ps.append(bank)
-
         b_grouped = sbuf.tile([P, NODES * PACK], BF16, align_bytes=64)
         b_codes = sbuf.tile([P, NODES], U32, align_bytes=64)
         b_scales = sbuf.tile([P, NODES], U8, align_bytes=64)
-        for c in range(2):
+        m_grouped = sbuf.tile([P, EMB, PACK], BF16, align_bytes=64)
+        m_codes = sbuf.tile([P, EMB], U32, align_bytes=64)
+        m_scales = sbuf.tile([P, EMB], U8, align_bytes=64)
+
+        def group_adj(copy, u, parts):
+            copy(
+                out=a_grouped[:, u * HALF * PACK : (u + 1) * HALF * PACK].rearrange(
+                    "p (s q j) -> p s q j", s=2, j=ROWS
+                )[:, parts],
+                in_=adj_raw[:, :, u * HALF : (u + 1) * HALF].rearrange("p j (q s) -> p s q j", s=2)[
+                    :, parts
+                ],
+            )
+
+        def group_e(copy, b):
+            f_cols = slice(b * P, (b + 1) * P)
+            copy(
+                out=e_grouped[:, f_cols, :].rearrange("p (c i) j -> p c j i", i=4),
+                in_=e_raw[:, :, f_cols].rearrange("p j (c i) -> p c j i", i=4),
+            )
+
+        def group_b(c):
             nc.scalar.copy(
                 out=b_grouped[:].bitcast(F32)[:, c * BANK : (c + 1) * BANK].rearrange(
                     "p (n u) -> p n u", u=2
@@ -138,33 +123,52 @@ def tile_hgnnmodel_pa_s_kernel(tc, e_nodes, adj, ego_embeddings, ln_gamma, ln_be
                 in_=adj_t[c][:].rearrange("p (u n) -> p n u", u=2),
             )
 
-        for c in range(2):
-            nc.vector.quantize_mx(
-                out=b_codes[:, c * 2 * P : (c + 1) * 2 * P].bitcast(FP8X4),
-                scales=b_scales[:, c * 2 * P : (c + 1) * 2 * P],
-                in_=b_grouped[:, c * 2 * P * PACK : (c + 1) * 2 * P * PACK],
+        def group_m(copy, b):
+            copy(
+                out=m_grouped[:, b * P : (b + 1) * P, :],
+                in_=m_ps[b][:].rearrange("p t f -> p f t"),
             )
 
-        m_grouped = sbuf.tile([P, EMB, PACK], BF16, align_bytes=64)
-        m_codes = sbuf.tile([P, EMB], U32, align_bytes=64)
-        m_scales = sbuf.tile([P, EMB], U8, align_bytes=64)
-        h_ps = [psum.tile([P, BANK], F32, name="h_ps%d" % j, tag="bank") for j in range(ROWS)]
-        shift = sbuf.tile([P, ROWS, EMB], F32)
-        for b in range(F_BLOCKS):
-            f_cols = slice(b * P, (b + 1) * P)
-            nc.scalar.copy(out=m_grouped[:, f_cols, :], in_=m_ps[b][:].rearrange("p t f -> p f t"))
+        def quantize(codes, scales, grouped, cols):
             nc.vector.quantize_mx(
-                out=m_codes[:, f_cols].bitcast(FP8X4),
-                scales=m_scales[:, f_cols],
-                in_=m_grouped[:, f_cols, :].rearrange("p f t -> p (f t)"),
+                out=codes[:, cols].bitcast(FP8X4), scales=scales[:, cols], in_=grouped
             )
-            if b < 2:
-                nc.vector.tensor_tensor(
-                    out=shift[:, b, :],
-                    in0=ego_raw[:, b, :],
-                    in1=gain_bias_ps[:, 1, 0:EMB],
-                    op=ALU.add,
+
+        def quantize_adj(u):
+            quantize(
+                a_codes,
+                a_scales,
+                a_grouped[:, u * HALF * PACK : (u + 1) * HALF * PACK],
+                slice(u * HALF, (u + 1) * HALF),
+            )
+
+        def quantize_block(codes, scales, grouped, b):
+            f_cols = slice(b * P, (b + 1) * P)
+            quantize(codes, scales, grouped[:, f_cols, :].rearrange("p f t -> p (f t)"), f_cols)
+
+        def quantize_b(c):
+            quantize(
+                b_codes,
+                b_scales,
+                b_grouped[:, c * 2 * P * PACK : (c + 1) * 2 * P * PACK],
+                slice(c * 2 * P, (c + 1) * 2 * P),
+            )
+
+        def multiply_m(b):
+            f_cols = slice(b * P, (b + 1) * P)
+            for t in range(PACK):
+                nc.tensor.matmul_mx(
+                    out=m_ps[b][:, t, :],
+                    lhsT=a_codes[:, t * P : (t + 1) * P].bitcast(FP8X4),
+                    lhsT_scale=a_scales[:, t * P : (t + 1) * P],
+                    rhs=e_codes[:, f_cols].bitcast(FP8X4),
+                    rhs_scale=e_scales[:, f_cols],
+                    start=True,
+                    stop=True,
                 )
+
+        def multiply_h(b):
+            f_cols = slice(b * P, (b + 1) * P)
             for j in range(ROWS):
                 nc.tensor.matmul_mx(
                     out=h_ps[j][:, f_cols],
@@ -176,9 +180,36 @@ def tile_hgnnmodel_pa_s_kernel(tc, e_nodes, adj, ego_embeddings, ln_gamma, ln_be
                     stop=True,
                 )
 
+        m_ps = [psum.tile([P, PACK, P], F32, name="m_ps%d" % b, tag="bank") for b in range(F_BLOCKS)]
+        group_adj(nc.vector.tensor_copy, 0, slice(0, 2))
+        group_adj(nc.vector.tensor_copy, 1, slice(0, 1))
+        group_adj(nc.scalar.copy, 1, slice(1, 2))
+        group_e(nc.vector.tensor_copy, 0)
+        group_e(nc.scalar.copy, 1)
+        group_e(nc.scalar.copy, 2)
+        group_b(0)
+        group_b(1)
+        quantize_adj(0)
+        quantize_adj(1)
+        for b in range(F_BLOCKS):
+            quantize_block(e_codes, e_scales, e_grouped, b)
+            multiply_m(b)
+        shift = sbuf.tile([P, ROWS, EMB], F32)
+        nc.vector.tensor_tensor(
+            out=shift[:, 0, :], in0=ego_raw[:, 0, :], in1=gain_bias_ps[:, 1, 0:EMB], op=ALU.add
+        )
+        group_m(nc.vector.tensor_copy, 0)
+        group_m(nc.scalar.copy, 1)
+        group_m(nc.scalar.copy, 2)
+        quantize_b(0)
+        quantize_b(1)
+        h_ps = [psum.tile([P, BANK], F32, name="h_ps%d" % j, tag="bank") for j in range(ROWS)]
+        for b in range(F_BLOCKS):
+            quantize_block(m_codes, m_scales, m_grouped, b)
+            multiply_h(b)
         gain_bias = sbuf.tile([P, 2, EMB], BF16)
         nc.scalar.copy(out=gain_bias[:], in_=gain_bias_ps[:, :, 0:EMB])
-        for j in range(2, ROWS):
+        for j in range(1, ROWS):
             nc.gpsimd.tensor_tensor(
                 out=shift[:, j, :], in0=ego_raw[:, j, :], in1=gain_bias[:, 1, :], op=ALU.add
             )

@@ -167,18 +167,24 @@ def tile_hgnnmodel_pa_s_kernel(tc, e_nodes, adj, ego_embeddings, ln_gamma, ln_be
                     stop=True,
                 )
 
-        def multiply_h(b):
+        def multiply_h(b, j, out_cols, start, stop):
             f_cols = slice(b * P, (b + 1) * P)
-            for j in range(ROWS):
-                nc.tensor.matmul_mx(
-                    out=h_ps[j][:, f_cols],
-                    lhsT=b_codes[:, j * P : (j + 1) * P].bitcast(FP8X4),
-                    lhsT_scale=b_scales[:, j * P : (j + 1) * P],
-                    rhs=m_codes[:, f_cols].bitcast(FP8X4),
-                    rhs_scale=m_scales[:, f_cols],
-                    start=True,
-                    stop=True,
-                )
+            nc.tensor.matmul_mx(
+                out=h_ps[j][:, out_cols],
+                lhsT=b_codes[:, j * P : (j + 1) * P].bitcast(FP8X4),
+                lhsT_scale=b_scales[:, j * P : (j + 1) * P],
+                rhs=m_codes[:, f_cols].bitcast(FP8X4),
+                rhs_scale=m_scales[:, f_cols],
+                start=start,
+                stop=stop,
+            )
+
+        def multiply_block(b, j):
+            multiply_h(b, j, slice(b * P, (b + 1) * P), True, True)
+
+        def multiply_sum(j):
+            for b in range(F_BLOCKS):
+                multiply_h(b, j, slice(EMB, EMB + P), b == 0, b == F_BLOCKS - 1)
 
         m_ps = [psum.tile([P, PACK, P], F32, name="m_ps%d" % b, tag="bank") for b in range(F_BLOCKS)]
         group_adj(nc.vector.tensor_copy, 0, slice(0, 2))
@@ -194,40 +200,28 @@ def tile_hgnnmodel_pa_s_kernel(tc, e_nodes, adj, ego_embeddings, ln_gamma, ln_be
         for b in range(F_BLOCKS):
             quantize_block(e_codes, e_scales, e_grouped, b)
             multiply_m(b)
-        shift = sbuf.tile([P, ROWS, EMB], F32)
-        nc.vector.tensor_tensor(
-            out=shift[:, 0, :], in0=ego_raw[:, 0, :], in1=gain_bias_ps[:, 1, 0:EMB], op=ALU.add
-        )
-        group_m(nc.vector.tensor_copy, 0)
-        group_m(nc.scalar.copy, 1)
-        group_m(nc.scalar.copy, 2)
-        quantize_b(0)
-        quantize_b(1)
-        h_ps = [psum.tile([P, BANK], F32, name="h_ps%d" % j, tag="bank") for j in range(ROWS)]
-        for b in range(F_BLOCKS):
-            quantize_block(m_codes, m_scales, m_grouped, b)
-            multiply_h(b)
         gain_bias = sbuf.tile([P, 2, EMB], BF16)
-        nc.scalar.copy(out=gain_bias[:], in_=gain_bias_ps[:, :, 0:EMB])
-        for j in range(1, ROWS):
-            nc.gpsimd.tensor_tensor(
-                out=shift[:, j, :], in0=ego_raw[:, j, :], in1=gain_bias[:, 1, :], op=ALU.add
-            )
+        shift = sbuf.tile([P, ROWS, EMB], F32)
 
+        def join_shift(engine, j, bias):
+            engine.tensor_tensor(out=shift[:, j, :], in0=ego_raw[:, j, :], in1=bias, op=ALU.add)
+
+        h_ps = [psum.tile([P, BANK], F32, name="h_ps%d" % j, tag="bank") for j in range(ROWS)]
         mean_var = sbuf.tile([P, 2], F32)
+        bn_parts = sbuf.tile([P, 6], F32)
         neg_mean = sbuf.tile([P, ROWS], F32)
         sq_sum = sbuf.tile([P, ROWS], F32)
         rstd = sbuf.tile([P, ROWS], F32)
-        h_scaled = sbuf.tile([P, ROWS, EMB], F32)
+        sums_scaled = sbuf.tile([P, ROWS, P], F32)
         squares = sbuf.tile([P, ROWS, EMB], F32)
         centred = sbuf.tile([P, ROWS, EMB], F32)
         result = sbuf.tile([P, ROWS, EMB], F32)
         out_rows = out.rearrange("(p j) f -> p j f", j=ROWS)
 
-        def mean_on_scalar(j):
+        def negative_mean(j):
             nc.scalar.activation(
-                out=h_scaled[:, j, :],
-                in_=h_ps[j][:, 0:EMB],
+                out=sums_scaled[:, j, :],
+                in_=h_ps[j][:, EMB : EMB + P],
                 func=ACT.Copy,
                 scale=-1.0 / EMB,
                 accum_out=neg_mean[:, j : j + 1],
@@ -236,11 +230,19 @@ def tile_hgnnmodel_pa_s_kernel(tc, e_nodes, adj, ego_embeddings, ln_gamma, ln_be
         def squares_on_scalar(j):
             nc.scalar.activation(
                 out=squares[:, j, :],
-                in_=h_scaled[:, j, :],
+                in_=h_ps[j][:, 0:EMB],
                 func=ACT.Square,
-                scale=-1.0 * EMB,
                 bias=neg_mean[:, j : j + 1],
                 accum_out=sq_sum[:, j : j + 1],
+            )
+
+        def inverse_std(j, spread, factor):
+            nc.scalar.activation(
+                out=rstd[:, j : j + 1],
+                in_=spread,
+                func=ACT.Abs_reciprocal_sqrt,
+                scale=factor,
+                bias=eps[:],
             )
 
         def centre(j, offset, op):
@@ -251,15 +253,6 @@ def tile_hgnnmodel_pa_s_kernel(tc, e_nodes, adj, ego_embeddings, ln_gamma, ln_be
                 in1=gain_bias[:, 0, :],
                 op0=op,
                 op1=ALU.mult,
-            )
-
-        def inverse_std(j, spread, factor):
-            nc.scalar.activation(
-                out=rstd[:, j : j + 1],
-                in_=spread,
-                func=ACT.Abs_reciprocal_sqrt,
-                scale=factor,
-                bias=eps[:],
             )
 
         def finish(j):
@@ -273,15 +266,36 @@ def tile_hgnnmodel_pa_s_kernel(tc, e_nodes, adj, ego_embeddings, ln_gamma, ln_be
             )
             nc.sync.dma_start(out=out_rows[:, j, :], in_=result[:, j, :])
 
-        bn_parts = sbuf.tile([P, 6], F32)
+        join_shift(nc.vector, 0, gain_bias_ps[:, 1, 0:EMB])
+        group_m(nc.vector.tensor_copy, 0)
+        group_m(nc.scalar.copy, 1)
+        group_m(nc.scalar.copy, 2)
+        quantize_b(0)
+        for b in range(F_BLOCKS):
+            quantize_block(m_codes, m_scales, m_grouped, b)
+            for j in (0, 1):
+                multiply_block(b, j)
+        multiply_sum(1)
+        quantize_b(1)
+        for j in (2, 3):
+            for b in range(F_BLOCKS):
+                multiply_block(b, j)
+            multiply_sum(j)
+        nc.scalar.copy(out=gain_bias[:], in_=gain_bias_ps[:, :, 0:EMB])
+        for j in range(1, ROWS):
+            join_shift(nc.gpsimd, j, gain_bias[:, 1, :])
         nc.vector.bn_stats(out=bn_parts[:], in_=h_ps[0][:, 0:EMB])
+        for j in range(1, ROWS):
+            negative_mean(j)
+        centre(1, neg_mean[:, 1:2], ALU.add)
         nc.vector.bn_aggr(out=mean_var[:], in_=bn_parts[:])
+        centre(2, neg_mean[:, 2:3], ALU.add)
         centre(0, mean_var[:, 0:1], ALU.subtract)
-        for j in range(1, ROWS):
-            mean_on_scalar(j)
-            centre(j, neg_mean[:, j : j + 1], ALU.add)
+        centre(3, neg_mean[:, 3:4], ALU.add)
+        squares_on_scalar(1)
+        inverse_std(1, sq_sum[:, 1:2], 1.0 / EMB)
         inverse_std(0, mean_var[:, 1:2], 1.0)
-        for j in range(1, ROWS):
+        for j in (2, 3):
             squares_on_scalar(j)
             inverse_std(j, sq_sum[:, j : j + 1], 1.0 / EMB)
         for j in range(ROWS):

@@ -75,10 +75,10 @@ def tile_hgnnmodel_pa_s_kernel(tc, e_nodes, adj, ego_embeddings, ln_gamma, ln_be
                         ident[:],
                     )
 
-        gain_bias_ps = psum.tile([P, 2, BANK], BF16, tag="bank")
+        gain_bias_ps = [psum.tile([P, BANK], BF16, name="row_ps%d" % g, tag="bank") for g in range(2)]
         for g in range(2):
             nc.tensor.matmul(
-                out=gain_bias_ps[:, g, 0:EMB],
+                out=gain_bias_ps[g][:, 0:EMB],
                 lhsT=all_ones[:],
                 rhs=gain_bias_row[:, g, :],
                 start=True,
@@ -266,23 +266,26 @@ def tile_hgnnmodel_pa_s_kernel(tc, e_nodes, adj, ego_embeddings, ln_gamma, ln_be
             )
             nc.sync.dma_start(out=out_rows[:, j, :], in_=result[:, j, :])
 
-        join_shift(nc.vector, 0, gain_bias_ps[:, 1, 0:EMB])
+        join_shift(nc.vector, 0, gain_bias_ps[1][:, 0:EMB])
         group_m(nc.vector.tensor_copy, 0)
         group_m(nc.scalar.copy, 1)
         group_m(nc.scalar.copy, 2)
         quantize_b(0)
         for b in range(F_BLOCKS):
+            if b == F_BLOCKS - 1:
+                quantize_b(1)
             quantize_block(m_codes, m_scales, m_grouped, b)
             for j in (0, 1):
                 multiply_block(b, j)
         multiply_sum(1)
-        quantize_b(1)
+        join_shift(nc.vector, 1, gain_bias_ps[1][:, 0:EMB])
         for j in (2, 3):
             for b in range(F_BLOCKS):
                 multiply_block(b, j)
             multiply_sum(j)
-        nc.scalar.copy(out=gain_bias[:], in_=gain_bias_ps[:, :, 0:EMB])
-        for j in range(1, ROWS):
+        for g in range(2):
+            nc.scalar.copy(out=gain_bias[:, g, :], in_=gain_bias_ps[g][:, 0:EMB])
+        for j in range(2, ROWS):
             join_shift(nc.gpsimd, j, gain_bias[:, 1, :])
         nc.vector.bn_stats(out=bn_parts[:], in_=h_ps[0][:, 0:EMB])
         for j in range(1, ROWS):

@@ -203,6 +203,9 @@ def tile_hgnnmodel_pa_s_kernel(tc, e_nodes, adj, ego_embeddings, ln_gamma, ln_be
         gain_bias = sbuf.tile([P, 2, EMB], BF16)
         shift = sbuf.tile([P, ROWS, EMB], F32)
 
+        def copy_row(g):
+            nc.scalar.copy(out=gain_bias[:, g, :], in_=gain_bias_ps[g][:, 0:EMB])
+
         def join_shift(engine, j, bias):
             engine.tensor_tensor(out=shift[:, j, :], in0=ego_raw[:, j, :], in1=bias, op=ALU.add)
 
@@ -278,13 +281,13 @@ def tile_hgnnmodel_pa_s_kernel(tc, e_nodes, adj, ego_embeddings, ln_gamma, ln_be
             for j in (0, 1):
                 multiply_block(b, j)
         multiply_sum(1)
+        copy_row(1)
         join_shift(nc.vector, 1, gain_bias_ps[1][:, 0:EMB])
         for j in (2, 3):
             for b in range(F_BLOCKS):
                 multiply_block(b, j)
             multiply_sum(j)
-        for g in range(2):
-            nc.scalar.copy(out=gain_bias[:, g, :], in_=gain_bias_ps[g][:, 0:EMB])
+        copy_row(0)
         for j in range(2, ROWS):
             join_shift(nc.gpsimd, j, gain_bias[:, 1, :])
         nc.vector.bn_stats(out=bn_parts[:], in_=h_ps[0][:, 0:EMB])

@@ -75,6 +75,7 @@ def tile_hgnnmodel_pa_s_kernel(tc, e_nodes, adj, ego_embeddings, ln_gamma, ln_be
                         ident[:],
                     )
 
+        m_ps = [psum.tile([P, PACK, P], F32, name="m_ps%d" % b, tag="bank") for b in range(F_BLOCKS)]
         gain_bias_ps = [psum.tile([P, BANK], BF16, name="row_ps%d" % g, tag="bank") for g in range(2)]
         for g in range(2):
             nc.tensor.matmul(
@@ -98,14 +99,15 @@ def tile_hgnnmodel_pa_s_kernel(tc, e_nodes, adj, ego_embeddings, ln_gamma, ln_be
         m_codes = sbuf.tile([P, EMB], U32, align_bytes=64)
         m_scales = sbuf.tile([P, EMB], U8, align_bytes=64)
 
-        def group_adj(copy, u, parts):
+        def group_adj(copy, t):
+            u, s = divmod(t, 2)
             copy(
-                out=a_grouped[:, u * HALF * PACK : (u + 1) * HALF * PACK].rearrange(
-                    "p (s q j) -> p s q j", s=2, j=ROWS
-                )[:, parts],
-                in_=adj_raw[:, :, u * HALF : (u + 1) * HALF].rearrange("p j (q s) -> p s q j", s=2)[
-                    :, parts
-                ],
+                out=a_grouped[:, t * P * PACK : (t + 1) * P * PACK].rearrange(
+                    "p (c i j) -> p c j i", i=4, j=ROWS
+                ),
+                in_=adj_raw[:, :, u * HALF : (u + 1) * HALF].rearrange(
+                    "p j (c i s) -> p s c j i", i=4, s=2
+                )[:, s],
             )
 
         def group_e(copy, b):
@@ -186,10 +188,9 @@ def tile_hgnnmodel_pa_s_kernel(tc, e_nodes, adj, ego_embeddings, ln_gamma, ln_be
             for b in range(F_BLOCKS):
                 multiply_h(b, j, slice(EMB, EMB + P), b == 0, b == F_BLOCKS - 1)
 
-        m_ps = [psum.tile([P, PACK, P], F32, name="m_ps%d" % b, tag="bank") for b in range(F_BLOCKS)]
-        group_adj(nc.vector.tensor_copy, 0, slice(0, 2))
-        group_adj(nc.vector.tensor_copy, 1, slice(0, 1))
-        group_adj(nc.scalar.copy, 1, slice(1, 2))
+        for t in range(PACK - 1):
+            group_adj(nc.vector.tensor_copy, t)
+        group_adj(nc.scalar.copy, PACK - 1)
         group_e(nc.vector.tensor_copy, 0)
         group_e(nc.scalar.copy, 1)
         group_e(nc.scalar.copy, 2)
@@ -277,6 +278,9 @@ def tile_hgnnmodel_pa_s_kernel(tc, e_nodes, adj, ego_embeddings, ln_gamma, ln_be
         for b in range(F_BLOCKS):
             if b == F_BLOCKS - 1:
                 quantize_b(1)
+                for j in (2, 3):
+                    for ready in range(b):
+                        multiply_block(ready, j)
             quantize_block(m_codes, m_scales, m_grouped, b)
             for j in (0, 1):
                 multiply_block(b, j)
@@ -284,8 +288,7 @@ def tile_hgnnmodel_pa_s_kernel(tc, e_nodes, adj, ego_embeddings, ln_gamma, ln_be
         copy_row(1)
         join_shift(nc.vector, 1, gain_bias_ps[1][:, 0:EMB])
         for j in (2, 3):
-            for b in range(F_BLOCKS):
-                multiply_block(b, j)
+            multiply_block(F_BLOCKS - 1, j)
             multiply_sum(j)
         copy_row(0)
         for j in range(2, ROWS):

@@ -259,16 +259,16 @@ def tile_hgnnmodel_pa_s_kernel(tc, e_nodes, adj, ego_embeddings, ln_gamma, ln_be
                 op1=ALU.mult,
             )
 
-        def finish(j):
+        def finish(j, f_cols):
             nc.vector.scalar_tensor_tensor(
-                out=result[:, j, :],
-                in0=centred[:, j, :],
+                out=result[:, j, f_cols],
+                in0=centred[:, j, f_cols],
                 scalar=rstd[:, j : j + 1],
-                in1=shift[:, j, :],
+                in1=shift[:, j, f_cols],
                 op0=ALU.mult,
                 op1=ALU.add,
             )
-            nc.sync.dma_start(out=out_rows[:, j, :], in_=result[:, j, :])
+            nc.sync.dma_start(out=out_rows[:, j, f_cols], in_=result[:, j, f_cols])
 
         join_shift(nc.vector, 0, gain_bias_ps[1][:, 0:EMB])
         group_m(nc.vector.tensor_copy, 0)
@@ -307,5 +307,7 @@ def tile_hgnnmodel_pa_s_kernel(tc, e_nodes, adj, ego_embeddings, ln_gamma, ln_be
         for j in (2, 3):
             squares_on_scalar(j)
             inverse_std(j, sq_sum[:, j : j + 1], 1.0 / EMB)
-        for j in range(ROWS):
-            finish(j)
+        for j in range(ROWS - 1):
+            finish(j, slice(0, EMB))
+        for piece in (slice(0, 2 * P), slice(2 * P, EMB)):
+            finish(ROWS - 1, piece)

import concourse.mybir as mybir
from concourse.masks import make_identity

BF16 = mybir.dt.bfloat16
F32 = mybir.dt.float32
U32 = mybir.dt.uint32
U8 = mybir.dt.uint8
FP8X4 = mybir.dt.float8_e4m3fn_x4
ACT = mybir.ActivationFunctionType
ALU = mybir.AluOpType

P = 128
PACK = 4
NODES = 512
EDGES = 512
EMB = 384
LN_EPS = 1e-5

ROWS = NODES // P
HALF = EDGES // 2
F_BLOCKS = EMB // P
WARM_UPS = 3
BANK = 512

FLOPS = 2 * 2 * NODES * EDGES * EMB


def tile_hgnnmodel_pa_s_kernel(tc, e_nodes, adj, ego_embeddings, ln_gamma, ln_beta, out):
    nc = tc.nc
    with tc.tile_pool(name="sbuf", bufs=1) as sbuf, tc.psum_pool(
        name="psum", bufs=8
    ) as psum, tc.manual_schedule():

        adj_raw = sbuf.tile([P, ROWS, EDGES], BF16)
        nc.sync.dma_start(out=adj_raw[:], in_=adj.rearrange("(p j) e -> p j e", j=ROWS))
        gain_bias_row = sbuf.tile([P, 2, EMB], BF16)
        nc.vector.memset(gain_bias_row[:].rearrange("p g f -> p (g f)").bitcast(F32), 0.0)
        nc.sync.dma_start(
            out=gain_bias_row[0:1, 0, :], in_=ln_gamma.rearrange("(o f) -> o f", o=1)
        )
        nc.sync.dma_start(
            out=gain_bias_row[0:1, 1, :], in_=ln_beta.rearrange("(o f) -> o f", o=1)
        )
        e_raw = sbuf.tile([P, ROWS, EMB], BF16)
        nc.sync.dma_start(out=e_raw[:], in_=e_nodes.rearrange("(p j) f -> p j f", j=ROWS))
        ego_raw = sbuf.tile([P, ROWS, EMB], BF16)
        nc.sync.dma_start(out=ego_raw[:], in_=ego_embeddings.rearrange("(p j) f -> p j f", j=ROWS))

        all_ones = sbuf.tile([P, P], BF16)
        nc.vector.memset(all_ones[:], 1.0)
        one = sbuf.tile([P, 1], F32)
        nc.vector.memset(one[:], 1.0)
        eps = sbuf.tile([P, 1], F32)
        nc.vector.tensor_scalar(out=eps[:], in0=one[:], scalar1=LN_EPS, scalar2=None, op0=ALU.mult)
        table_warm = sbuf.tile([P, 1], F32)
        nc.scalar.activation(out=table_warm[:], in_=one[:], func=ACT.Abs_reciprocal_sqrt)
        ident = sbuf.tile([P, P], F32)
        make_identity(nc, ident[:])

        warm_ps = psum.tile([P, BANK], F32, tag="bank")
        for i in range(WARM_UPS):
            nc.tensor.matmul(
                out=warm_ps[:, i * P : (i + 1) * P], lhsT=ident[:], rhs=ident[:], start=True, stop=True
            )

        adj_words = adj_raw[:].rearrange("p j e -> p (j e)").bitcast(F32)
        adj_t = [psum.tile([P, BANK], F32, name="adj_t%d" % c, tag="bank") for c in range(2)]
        for c in range(2):
            for u in range(2):
                for i in range(2):
                    j = 2 * c + i
                    nc.tensor.transpose(
                        adj_t[c][:, (2 * u + i) * P : (2 * u + i + 1) * P],
                        adj_words[:, (2 * j + u) * P : (2 * j + u + 1) * P],
                        ident[:],
                    )

        m_ps = [psum.tile([P, PACK, P], F32, name="m_ps%d" % b, tag="bank") for b in range(F_BLOCKS)]
        gain_bias_ps = [psum.tile([P, BANK], BF16, name="row_ps%d" % g, tag="bank") for g in range(2)]
        for g in range(2):
            nc.tensor.matmul(
                out=gain_bias_ps[g][:, 0:EMB],
                lhsT=all_ones[:],
                rhs=gain_bias_row[:, g, :],
                start=True,
                stop=True,
            )

        a_grouped = sbuf.tile([P, EDGES * PACK], BF16, align_bytes=64)
        a_codes = sbuf.tile([P, EDGES], U32, align_bytes=64)
        a_scales = sbuf.tile([P, EDGES], U8, align_bytes=64)
        e_grouped = sbuf.tile([P, EMB, PACK], BF16, align_bytes=64)
        e_codes = sbuf.tile([P, EMB], U32, align_bytes=64)
        e_scales = sbuf.tile([P, EMB], U8, align_bytes=64)
        b_grouped = sbuf.tile([P, NODES * PACK], BF16, align_bytes=64)
        b_codes = sbuf.tile([P, NODES], U32, align_bytes=64)
        b_scales = sbuf.tile([P, NODES], U8, align_bytes=64)
        m_grouped = sbuf.tile([P, EMB, PACK], BF16, align_bytes=64)
        m_codes = sbuf.tile([P, EMB], U32, align_bytes=64)
        m_scales = sbuf.tile([P, EMB], U8, align_bytes=64)

        def group_adj(copy, t):
            u, s = divmod(t, 2)
            copy(
                out=a_grouped[:, t * P * PACK : (t + 1) * P * PACK].rearrange(
                    "p (c i j) -> p c j i", i=4, j=ROWS
                ),
                in_=adj_raw[:, :, u * HALF : (u + 1) * HALF].rearrange(
                    "p j (c i s) -> p s c j i", i=4, s=2
                )[:, s],
            )

        def group_e(copy, b):
            f_cols = slice(b * P, (b + 1) * P)
            copy(
                out=e_grouped[:, f_cols, :].rearrange("p (c i) j -> p c j i", i=4),
                in_=e_raw[:, :, f_cols].rearrange("p j (c i) -> p c j i", i=4),
            )

        def group_b(c):
            nc.scalar.copy(
                out=b_grouped[:].bitcast(F32)[:, c * BANK : (c + 1) * BANK].rearrange(
                    "p (n u) -> p n u", u=2
                ),
                in_=adj_t[c][:].rearrange("p (u n) -> p n u", u=2),
            )

        def group_m(copy, b):
            copy(
                out=m_grouped[:, b * P : (b + 1) * P, :],
                in_=m_ps[b][:].rearrange("p t f -> p f t"),
            )

        def quantize(codes, scales, grouped, cols):
            nc.vector.quantize_mx(
                out=codes[:, cols].bitcast(FP8X4), scales=scales[:, cols], in_=grouped
            )

        def quantize_adj(u):
            quantize(
                a_codes,
                a_scales,
                a_grouped[:, u * HALF * PACK : (u + 1) * HALF * PACK],
                slice(u * HALF, (u + 1) * HALF),
            )

        def quantize_block(codes, scales, grouped, b):
            f_cols = slice(b * P, (b + 1) * P)
            quantize(codes, scales, grouped[:, f_cols, :].rearrange("p f t -> p (f t)"), f_cols)

        def quantize_b(c):
            quantize(
                b_codes,
                b_scales,
                b_grouped[:, c * 2 * P * PACK : (c + 1) * 2 * P * PACK],
                slice(c * 2 * P, (c + 1) * 2 * P),
            )

        def multiply_m(b):
            f_cols = slice(b * P, (b + 1) * P)
            for t in range(PACK):
                nc.tensor.matmul_mx(
                    out=m_ps[b][:, t, :],
                    lhsT=a_codes[:, t * P : (t + 1) * P].bitcast(FP8X4),
                    lhsT_scale=a_scales[:, t * P : (t + 1) * P],
                    rhs=e_codes[:, f_cols].bitcast(FP8X4),
                    rhs_scale=e_scales[:, f_cols],
                    start=True,
                    stop=True,
                )

        def multiply_h(b, j, out_cols, start, stop):
            f_cols = slice(b * P, (b + 1) * P)
            nc.tensor.matmul_mx(
                out=h_ps[j][:, out_cols],
                lhsT=b_codes[:, j * P : (j + 1) * P].bitcast(FP8X4),
                lhsT_scale=b_scales[:, j * P : (j + 1) * P],
                rhs=m_codes[:, f_cols].bitcast(FP8X4),
                rhs_scale=m_scales[:, f_cols],
                start=start,
                stop=stop,
            )

        def multiply_block(b, j):
            multiply_h(b, j, slice(b * P, (b + 1) * P), True, True)

        def multiply_sum(j):
            for b in range(F_BLOCKS):
                multiply_h(b, j, slice(EMB, EMB + P), b == 0, b == F_BLOCKS - 1)

        for t in range(PACK - 1):
            group_adj(nc.vector.tensor_copy, t)
        group_adj(nc.scalar.copy, PACK - 1)
        group_e(nc.vector.tensor_copy, 0)
        group_e(nc.scalar.copy, 1)
        group_e(nc.scalar.copy, 2)
        group_b(0)
        group_b(1)
        quantize_adj(0)
        quantize_adj(1)
        for b in range(F_BLOCKS):
            quantize_block(e_codes, e_scales, e_grouped, b)
            multiply_m(b)
        gain_bias = sbuf.tile([P, 2, EMB], BF16)
        shift = sbuf.tile([P, ROWS, EMB], F32)

        def copy_row(g):
            nc.scalar.copy(out=gain_bias[:, g, :], in_=gain_bias_ps[g][:, 0:EMB])

        def join_shift(engine, j, bias):
            engine.tensor_tensor(out=shift[:, j, :], in0=ego_raw[:, j, :], in1=bias, op=ALU.add)

        h_ps = [psum.tile([P, BANK], F32, name="h_ps%d" % j, tag="bank") for j in range(ROWS)]
        mean_var = sbuf.tile([P, 2], F32)
        bn_parts = sbuf.tile([P, 6], F32)
        neg_mean = sbuf.tile([P, ROWS], F32)
        sq_sum = sbuf.tile([P, ROWS], F32)
        rstd = sbuf.tile([P, ROWS], F32)
        sums_scaled = sbuf.tile([P, ROWS, P], F32)
        squares = sbuf.tile([P, ROWS, EMB], F32)
        centred = sbuf.tile([P, ROWS, EMB], F32)
        result = sbuf.tile([P, ROWS, EMB], F32)
        out_rows = out.rearrange("(p j) f -> p j f", j=ROWS)

        def negative_mean(j):
            nc.scalar.activation(
                out=sums_scaled[:, j, :],
                in_=h_ps[j][:, EMB : EMB + P],
                func=ACT.Copy,
                scale=-1.0 / EMB,
                accum_out=neg_mean[:, j : j + 1],
            )

        def squares_on_scalar(j):
            nc.scalar.activation(
                out=squares[:, j, :],
                in_=h_ps[j][:, 0:EMB],
                func=ACT.Square,
                bias=neg_mean[:, j : j + 1],
                accum_out=sq_sum[:, j : j + 1],
            )

        def inverse_std(j, spread, factor):
            nc.scalar.activation(
                out=rstd[:, j : j + 1],
                in_=spread,
                func=ACT.Abs_reciprocal_sqrt,
                scale=factor,
                bias=eps[:],
            )

        def centre(j, offset, op):
            nc.vector.scalar_tensor_tensor(
                out=centred[:, j, :],
                in0=h_ps[j][:, 0:EMB],
                scalar=offset,
                in1=gain_bias[:, 0, :],
                op0=op,
                op1=ALU.mult,
            )

        def finish(j, f_cols):
            nc.vector.scalar_tensor_tensor(
                out=result[:, j, f_cols],
                in0=centred[:, j, f_cols],
                scalar=rstd[:, j : j + 1],
                in1=shift[:, j, f_cols],
                op0=ALU.mult,
                op1=ALU.add,
            )
            nc.sync.dma_start(out=out_rows[:, j, f_cols], in_=result[:, j, f_cols])

        join_shift(nc.vector, 0, gain_bias_ps[1][:, 0:EMB])
        group_m(nc.vector.tensor_copy, 0)
        group_m(nc.scalar.copy, 1)
        group_m(nc.scalar.copy, 2)
        quantize_b(0)
        for b in range(F_BLOCKS):
            if b == F_BLOCKS - 1:
                quantize_b(1)
                for j in (2, 3):
                    for ready in range(b):
                        multiply_block(ready, j)
            quantize_block(m_codes, m_scales, m_grouped, b)
            for j in (0, 1):
                multiply_block(b, j)
        multiply_sum(1)
        copy_row(1)
        join_shift(nc.vector, 1, gain_bias_ps[1][:, 0:EMB])
        for j in (2, 3):
            multiply_block(F_BLOCKS - 1, j)
            multiply_sum(j)
        copy_row(0)
        for j in range(2, ROWS):
            join_shift(nc.gpsimd, j, gain_bias[:, 1, :])
        nc.vector.bn_stats(out=bn_parts[:], in_=h_ps[0][:, 0:EMB])
        for j in range(1, ROWS):
            negative_mean(j)
        centre(1, neg_mean[:, 1:2], ALU.add)
        nc.vector.bn_aggr(out=mean_var[:], in_=bn_parts[:])
        centre(2, neg_mean[:, 2:3], ALU.add)
        centre(0, mean_var[:, 0:1], ALU.subtract)
        centre(3, neg_mean[:, 3:4], ALU.add)
        squares_on_scalar(1)
        inverse_std(1, sq_sum[:, 1:2], 1.0 / EMB)
        inverse_std(0, mean_var[:, 1:2], 1.0)
        for j in (2, 3):
            squares_on_scalar(j)
            inverse_std(j, sq_sum[:, j : j + 1], 1.0 / EMB)
        for j in range(ROWS - 1):
            finish(j, slice(0, EMB))
        for piece in (slice(0, 2 * P), slice(2 * P, EMB)):
            finish(ROWS - 1, piece)
